import numpy as np
import ml_dtypes

BF16 = ml_dtypes.bfloat16


def bf(x):
    return np.asarray(x, np.float32).astype(BF16)


def f32(x):
    return np.asarray(x, np.float32)


def f64(x):
    return np.asarray(x).astype(np.float64)


def striped(idx):
    return np.tile(idx.reshape(-1, 16).T, (8, 1))


S, D, M, E, T, N = 4096, 128, 128, 64, 32, 2048


def setup_inputs():
    return {
        "table": bf(np.random.standard_normal((D, S))),
        "w": bf(np.random.standard_normal((D, M)) / np.sqrt(D)),
        "wpos": f32(0.5 * np.random.standard_normal((M, T))),
        "b": f32(0.3 * np.random.standard_normal((M, 1))),
        "mask": f32(0.5 + np.random.random((1, N))),
        "offs": striped(np.random.permutation(np.tile(np.arange(S), 2))[:N]),
    }


def reference(table, w, wpos, b, mask, offs):
    idx = offs[:16].T.reshape(-1)
    pre = f64(w).T @ f64(table)[:, idx] + np.tile(f64(wpos), (1, E)) + f64(b)
    return f64(mask) * np.maximum(pre, 0.0)

@@ -1,0 +1,67 @@
+import concourse.mybir as mybir
+
+BF16, F32, U16 = mybir.dt.bfloat16, mybir.dt.float32, mybir.dt.uint16
+ADD, MAX, MULT = mybir.AluOpType.add, mybir.AluOpType.max, mybir.AluOpType.mult
+
+P = 128
+WORDS = 4096
+N = 2048
+POSITIONS = 32
+PIECE = 512
+PIECES = N // PIECE
+GOALS = PIECE // POSITIONS
+LANES = 16
+
+FLOPS = 2 * P * P * N
+
+
+def tile_domleavesembedding_kernel(tc, table, w, wpos, b, mask, offs, out):
+    nc = tc.nc
+    with (
+        tc.tile_pool(name="held", bufs=1) as held,
+        tc.tile_pool(name="work", bufs=2) as work,
+        tc.psum_pool(name="banks", bufs=PIECES) as banks,
+    ):
+        offsets = held.tile([P, N // LANES], U16, name="offsets")
+        nc.sync.dma_start(offsets[:], offs)
+        words = held.tile([P, WORDS], BF16, name="words")
+        nc.sync.dma_start(words[:], table)
+
+        weights = held.tile([P, P], BF16, name="weights")
+        nc.scalar.dma_start(weights[:], w)
+        position = held.tile([P, POSITIONS], F32, name="position")
+        nc.scalar.dma_start(position[:], wpos)
+        bias = held.tile([P, 1], F32, name="bias")
+        nc.scalar.dma_start(bias[:], b)
+
+        mask_rows = held.tile([P, N], F32, name="mask_rows")
+        for i in range(PIECES):
+            cols = slice(i * PIECE, (i + 1) * PIECE)
+            nc.sync.dma_start(mask_rows[:, cols], mask[:, cols].to_broadcast([P, PIECE]))
+
+        position_per_goal = position[:].unsqueeze(1).to_broadcast([P, GOALS, POSITIONS])
+
+        for i in range(PIECES):
+            cols = slice(i * PIECE, (i + 1) * PIECE)
+
+            picked = words[:].indirect(offsets[:, i * PIECE // LANES : (i + 1) * PIECE // LANES])
+            product = banks.tile([P, PIECE], F32, name="product")
+            nc.tensor.matmul(product[:], weights[:], picked, start=True, stop=True)
+
+            pre = work.tile([P, PIECE], F32, name="pre")
+            nc.vector.scalar_tensor_tensor(
+                out=pre[:].rearrange("p (g t) -> p g t", t=POSITIONS),
+                in0=product[:].rearrange("p (g t) -> p g t", t=POSITIONS),
+                scalar=bias[:, 0:1],
+                in1=position_per_goal,
+                op0=ADD,
+                op1=ADD,
+            )
+
+            result = work.tile([P, PIECE], F32, name="result")
+            nc.vector.scalar_tensor_tensor(
+                out=result[:], in0=pre[:], scalar=0.0, in1=mask_rows[:, cols], op0=MAX, op1=MULT
+            )
+
+            queue = nc.sync if i % 2 == 0 else nc.scalar
+            queue.dma_start(out[:, cols], result[:])

@@ -19,7 +19,7 @@ def tile_domleavesembedding_kernel(tc, table, w, wpos, b, mask, offs, out):
     nc = tc.nc
     with (
         tc.tile_pool(name="held", bufs=1) as held,
-        tc.tile_pool(name="work", bufs=2) as work,
+        tc.tile_pool(name="work", bufs=PIECES) as work,
         tc.psum_pool(name="banks", bufs=PIECES) as banks,
     ):
         offsets = held.tile([P, N // LANES], U16, name="offsets")

@@ -2,15 +2,19 @@ import concourse.mybir as mybir
 
 BF16, F32, U16 = mybir.dt.bfloat16, mybir.dt.float32, mybir.dt.uint16
 ADD, MAX, MULT = mybir.AluOpType.add, mybir.AluOpType.max, mybir.AluOpType.mult
+RELU = mybir.ActivationFunctionType.Relu
 
 P = 128
 WORDS = 4096
 N = 2048
 POSITIONS = 32
-PIECE = 512
+PIECE = 256
 PIECES = N // PIECE
 GOALS = PIECE // POSITIONS
 LANES = 16
+MASK_LOAD = 512
+BANK = 512
+WARM_MATMULS = 8
 
 FLOPS = 2 * P * P * N
 
@@ -20,7 +24,7 @@ def tile_domleavesembedding_kernel(tc, table, w, wpos, b, mask, offs, out):
     with (
         tc.tile_pool(name="held", bufs=1) as held,
         tc.tile_pool(name="work", bufs=PIECES) as work,
-        tc.psum_pool(name="banks", bufs=PIECES) as banks,
+        tc.psum_pool(name="banks", bufs=4) as banks,
     ):
         offsets = held.tile([P, N // LANES], U16, name="offsets")
         nc.sync.dma_start(offsets[:], offs)
@@ -35,9 +39,15 @@ def tile_domleavesembedding_kernel(tc, table, w, wpos, b, mask, offs, out):
         nc.scalar.dma_start(bias[:], b)
 
         mask_rows = held.tile([P, N], F32, name="mask_rows")
-        for i in range(PIECES):
-            cols = slice(i * PIECE, (i + 1) * PIECE)
-            nc.sync.dma_start(mask_rows[:, cols], mask[:, cols].to_broadcast([P, PIECE]))
+        for first in range(0, N, MASK_LOAD):
+            cols = slice(first, first + MASK_LOAD)
+            nc.sync.dma_start(mask_rows[:, cols], mask[:, cols].to_broadcast([P, MASK_LOAD]))
+
+        zeros = held.tile([P, BANK], BF16, name="zeros")
+        nc.vector.memset(zeros[:], 0.0)
+        unread = banks.tile([P, BANK], F32, name="unread", bufs=1)
+        for turn in range(WARM_MATMULS):
+            nc.tensor.matmul(unread[:], zeros[:, :P], zeros[:], start=True, stop=True)
 
         position_per_goal = position[:].unsqueeze(1).to_broadcast([P, GOALS, POSITIONS])
 
@@ -59,9 +69,14 @@ def tile_domleavesembedding_kernel(tc, table, w, wpos, b, mask, offs, out):
             )
 
             result = work.tile([P, PIECE], F32, name="result")
-            nc.vector.scalar_tensor_tensor(
-                out=result[:], in0=pre[:], scalar=0.0, in1=mask_rows[:, cols], op0=MAX, op1=MULT
-            )
+            if i % 2 == 1:
+                nc.vector.scalar_tensor_tensor(
+                    out=result[:], in0=pre[:], scalar=0.0, in1=mask_rows[:, cols], op0=MAX, op1=MULT
+                )
+            else:
+                positive = work.tile([P, PIECE], F32, name="positive")
+                nc.scalar.activation(positive[:], pre[:], RELU)
+                nc.gpsimd.tensor_tensor(result[:], positive[:], mask_rows[:, cols], MULT)
 
             queue = nc.sync if i % 2 == 0 else nc.scalar
             queue.dma_start(out[:, cols], result[:])

@@ -2,19 +2,15 @@ import concourse.mybir as mybir
 
 BF16, F32, U16 = mybir.dt.bfloat16, mybir.dt.float32, mybir.dt.uint16
 ADD, MAX, MULT = mybir.AluOpType.add, mybir.AluOpType.max, mybir.AluOpType.mult
-RELU = mybir.ActivationFunctionType.Relu
 
 P = 128
 WORDS = 4096
 N = 2048
 POSITIONS = 32
-PIECE = 256
+PIECE = 512
 PIECES = N // PIECE
 GOALS = PIECE // POSITIONS
 LANES = 16
-MASK_LOAD = 512
-BANK = 512
-WARM_MATMULS = 8
 
 FLOPS = 2 * P * P * N
 
@@ -24,30 +20,24 @@ def tile_domleavesembedding_kernel(tc, table, w, wpos, b, mask, offs, out):
     with (
         tc.tile_pool(name="held", bufs=1) as held,
         tc.tile_pool(name="work", bufs=PIECES) as work,
-        tc.psum_pool(name="banks", bufs=4) as banks,
+        tc.psum_pool(name="banks", bufs=PIECES) as banks,
     ):
         offsets = held.tile([P, N // LANES], U16, name="offsets")
         nc.sync.dma_start(offsets[:], offs)
         words = held.tile([P, WORDS], BF16, name="words")
         nc.sync.dma_start(words[:], table)
 
-        weights = held.tile([P, P], BF16, name="weights")
-        nc.scalar.dma_start(weights[:], w)
-        position = held.tile([P, POSITIONS], F32, name="position")
-        nc.scalar.dma_start(position[:], wpos)
-        bias = held.tile([P, 1], F32, name="bias")
-        nc.scalar.dma_start(bias[:], b)
-
         mask_rows = held.tile([P, N], F32, name="mask_rows")
-        for first in range(0, N, MASK_LOAD):
-            cols = slice(first, first + MASK_LOAD)
-            nc.sync.dma_start(mask_rows[:, cols], mask[:, cols].to_broadcast([P, MASK_LOAD]))
+        for i in range(PIECES):
+            cols = slice(i * PIECE, (i + 1) * PIECE)
+            nc.scalar.dma_start(mask_rows[:, cols], mask[:, cols].to_broadcast([P, PIECE]))
 
-        zeros = held.tile([P, BANK], BF16, name="zeros")
-        nc.vector.memset(zeros[:], 0.0)
-        unread = banks.tile([P, BANK], F32, name="unread", bufs=1)
-        for turn in range(WARM_MATMULS):
-            nc.tensor.matmul(unread[:], zeros[:, :P], zeros[:], start=True, stop=True)
+        weights = held.tile([P, P], BF16, name="weights")
+        nc.gpsimd.dma_start(weights[:], w)
+        position = held.tile([P, POSITIONS], F32, name="position")
+        nc.gpsimd.dma_start(position[:], wpos)
+        bias = held.tile([P, 1], F32, name="bias")
+        nc.gpsimd.dma_start(bias[:], b)
 
         position_per_goal = position[:].unsqueeze(1).to_broadcast([P, GOALS, POSITIONS])
 
@@ -69,14 +59,9 @@ def tile_domleavesembedding_kernel(tc, table, w, wpos, b, mask, offs, out):
             )
 
             result = work.tile([P, PIECE], F32, name="result")
-            if i % 2 == 1:
-                nc.vector.scalar_tensor_tensor(
-                    out=result[:], in0=pre[:], scalar=0.0, in1=mask_rows[:, cols], op0=MAX, op1=MULT
-                )
-            else:
-                positive = work.tile([P, PIECE], F32, name="positive")
-                nc.scalar.activation(positive[:], pre[:], RELU)
-                nc.gpsimd.tensor_tensor(result[:], positive[:], mask_rows[:, cols], MULT)
+            nc.vector.scalar_tensor_tensor(
+                out=result[:], in0=pre[:], scalar=0.0, in1=mask_rows[:, cols], op0=MAX, op1=MULT
+            )
 
             queue = nc.sync if i % 2 == 0 else nc.scalar
             queue.dma_start(out[:, cols], result[:])

@@ -2,6 +2,7 @@ import concourse.mybir as mybir
 
 BF16, F32, U16 = mybir.dt.bfloat16, mybir.dt.float32, mybir.dt.uint16
 ADD, MAX, MULT = mybir.AluOpType.add, mybir.AluOpType.max, mybir.AluOpType.mult
+RELU = mybir.ActivationFunctionType.Relu
 
 P = 128
 WORDS = 4096
@@ -27,17 +28,17 @@ def tile_domleavesembedding_kernel(tc, table, w, wpos, b, mask, offs, out):
         words = held.tile([P, WORDS], BF16, name="words")
         nc.sync.dma_start(words[:], table)
 
+        weights = held.tile([P, P], BF16, name="weights")
+        nc.scalar.dma_start(weights[:], w)
+        position = held.tile([P, POSITIONS], F32, name="position")
+        nc.scalar.dma_start(position[:], wpos)
+        bias = held.tile([P, 1], F32, name="bias")
+        nc.scalar.dma_start(bias[:], b)
+
         mask_rows = held.tile([P, N], F32, name="mask_rows")
         for i in range(PIECES):
             cols = slice(i * PIECE, (i + 1) * PIECE)
-            nc.scalar.dma_start(mask_rows[:, cols], mask[:, cols].to_broadcast([P, PIECE]))
-
-        weights = held.tile([P, P], BF16, name="weights")
-        nc.gpsimd.dma_start(weights[:], w)
-        position = held.tile([P, POSITIONS], F32, name="position")
-        nc.gpsimd.dma_start(position[:], wpos)
-        bias = held.tile([P, 1], F32, name="bias")
-        nc.gpsimd.dma_start(bias[:], b)
+            nc.sync.dma_start(mask_rows[:, cols], mask[:, cols].to_broadcast([P, PIECE]))
 
         position_per_goal = position[:].unsqueeze(1).to_broadcast([P, GOALS, POSITIONS])
 
@@ -59,9 +60,14 @@ def tile_domleavesembedding_kernel(tc, table, w, wpos, b, mask, offs, out):
             )
 
             result = work.tile([P, PIECE], F32, name="result")
-            nc.vector.scalar_tensor_tensor(
-                out=result[:], in0=pre[:], scalar=0.0, in1=mask_rows[:, cols], op0=MAX, op1=MULT
-            )
+            if i < PIECES // 2:
+                positive = work.tile([P, PIECE], F32, name="positive")
+                nc.scalar.activation(positive[:], pre[:], RELU)
+                nc.gpsimd.tensor_tensor(result[:], positive[:], mask_rows[:, cols], MULT)
+            else:
+                nc.vector.scalar_tensor_tensor(
+                    out=result[:], in0=pre[:], scalar=0.0, in1=mask_rows[:, cols], op0=MAX, op1=MULT
+                )
 
             queue = nc.sync if i % 2 == 0 else nc.scalar
             queue.dma_start(out[:, cols], result[:])

@@ -2,16 +2,16 @@ import concourse.mybir as mybir
 
 BF16, F32, U16 = mybir.dt.bfloat16, mybir.dt.float32, mybir.dt.uint16
 ADD, MAX, MULT = mybir.AluOpType.add, mybir.AluOpType.max, mybir.AluOpType.mult
-RELU = mybir.ActivationFunctionType.Relu
 
 P = 128
 WORDS = 4096
 N = 2048
 POSITIONS = 32
-PIECE = 512
+PIECE = 256
 PIECES = N // PIECE
 GOALS = PIECE // POSITIONS
 LANES = 16
+MASK_LOAD = 512
 
 FLOPS = 2 * P * P * N
 
@@ -36,9 +36,9 @@ def tile_domleavesembedding_kernel(tc, table, w, wpos, b, mask, offs, out):
         nc.scalar.dma_start(bias[:], b)
 
         mask_rows = held.tile([P, N], F32, name="mask_rows")
-        for i in range(PIECES):
-            cols = slice(i * PIECE, (i + 1) * PIECE)
-            nc.sync.dma_start(mask_rows[:, cols], mask[:, cols].to_broadcast([P, PIECE]))
+        for first in range(0, N, MASK_LOAD):
+            cols = slice(first, first + MASK_LOAD)
+            nc.sync.dma_start(mask_rows[:, cols], mask[:, cols].to_broadcast([P, MASK_LOAD]))
 
         position_per_goal = position[:].unsqueeze(1).to_broadcast([P, GOALS, POSITIONS])
 
@@ -60,14 +60,9 @@ def tile_domleavesembedding_kernel(tc, table, w, wpos, b, mask, offs, out):
             )
 
             result = work.tile([P, PIECE], F32, name="result")
-            if i < PIECES // 2:
-                positive = work.tile([P, PIECE], F32, name="positive")
-                nc.scalar.activation(positive[:], pre[:], RELU)
-                nc.gpsimd.tensor_tensor(result[:], positive[:], mask_rows[:, cols], MULT)
-            else:
-                nc.vector.scalar_tensor_tensor(
-                    out=result[:], in0=pre[:], scalar=0.0, in1=mask_rows[:, cols], op0=MAX, op1=MULT
-                )
+            nc.vector.scalar_tensor_tensor(
+                out=result[:], in0=pre[:], scalar=0.0, in1=mask_rows[:, cols], op0=MAX, op1=MULT
+            )
 
             queue = nc.sync if i % 2 == 0 else nc.scalar
             queue.dma_start(out[:, cols], result[:])

@@ -7,11 +7,11 @@ P = 128
 WORDS = 4096
 N = 2048
 POSITIONS = 32
-PIECE = 256
+PIECE = 512
 PIECES = N // PIECE
 GOALS = PIECE // POSITIONS
 LANES = 16
-MASK_LOAD = 512
+WARM_MATMULS = 6
 
 FLOPS = 2 * P * P * N
 
@@ -36,9 +36,15 @@ def tile_domleavesembedding_kernel(tc, table, w, wpos, b, mask, offs, out):
         nc.scalar.dma_start(bias[:], b)
 
         mask_rows = held.tile([P, N], F32, name="mask_rows")
-        for first in range(0, N, MASK_LOAD):
-            cols = slice(first, first + MASK_LOAD)
-            nc.sync.dma_start(mask_rows[:, cols], mask[:, cols].to_broadcast([P, MASK_LOAD]))
+        for i in range(PIECES):
+            cols = slice(i * PIECE, (i + 1) * PIECE)
+            nc.sync.dma_start(mask_rows[:, cols], mask[:, cols].to_broadcast([P, PIECE]))
+
+        zeros = held.tile([P, PIECE], BF16, name="zeros")
+        nc.vector.memset(zeros[:], 0.0)
+        unread = banks.tile([P, PIECE], F32, name="unread", bufs=1)
+        for turn in range(WARM_MATMULS):
+            nc.tensor.matmul(unread[:], zeros[:, :P], zeros[:], start=True, stop=True)
 
         position_per_goal = position[:].unsqueeze(1).to_broadcast([P, GOALS, POSITIONS])
 

@@ -11,7 +11,7 @@ PIECE = 512
 PIECES = N // PIECE
 GOALS = PIECE // POSITIONS
 LANES = 16
-WARM_MATMULS = 6
+MASK_LOAD = 1024
 
 FLOPS = 2 * P * P * N
 
@@ -36,15 +36,9 @@ def tile_domleavesembedding_kernel(tc, table, w, wpos, b, mask, offs, out):
         nc.scalar.dma_start(bias[:], b)
 
         mask_rows = held.tile([P, N], F32, name="mask_rows")
-        for i in range(PIECES):
-            cols = slice(i * PIECE, (i + 1) * PIECE)
-            nc.sync.dma_start(mask_rows[:, cols], mask[:, cols].to_broadcast([P, PIECE]))
-
-        zeros = held.tile([P, PIECE], BF16, name="zeros")
-        nc.vector.memset(zeros[:], 0.0)
-        unread = banks.tile([P, PIECE], F32, name="unread", bufs=1)
-        for turn in range(WARM_MATMULS):
-            nc.tensor.matmul(unread[:], zeros[:, :P], zeros[:], start=True, stop=True)
+        for first in range(0, N, MASK_LOAD):
+            cols = slice(first, first + MASK_LOAD)
+            nc.sync.dma_start(mask_rows[:, cols], mask[:, cols].to_broadcast([P, MASK_LOAD]))
 
         position_per_goal = position[:].unsqueeze(1).to_broadcast([P, GOALS, POSITIONS])
 

@@ -42,9 +42,8 @@ def tile_domleavesembedding_kernel(tc, table, w, wpos, b, mask, offs, out):
 
         position_per_goal = position[:].unsqueeze(1).to_broadcast([P, GOALS, POSITIONS])
 
+        pres = []
         for i in range(PIECES):
-            cols = slice(i * PIECE, (i + 1) * PIECE)
-
             picked = words[:].indirect(offsets[:, i * PIECE // LANES : (i + 1) * PIECE // LANES])
             product = banks.tile([P, PIECE], F32, name="product")
             nc.tensor.matmul(product[:], weights[:], picked, start=True, stop=True)
@@ -58,10 +57,14 @@ def tile_domleavesembedding_kernel(tc, table, w, wpos, b, mask, offs, out):
                 op0=ADD,
                 op1=ADD,
             )
+            pres.append(pre)
+
+        for i in range(PIECES):
+            cols = slice(i * PIECE, (i + 1) * PIECE)
 
             result = work.tile([P, PIECE], F32, name="result")
             nc.vector.scalar_tensor_tensor(
-                out=result[:], in0=pre[:], scalar=0.0, in1=mask_rows[:, cols], op0=MAX, op1=MULT
+                out=result[:], in0=pres[i][:], scalar=0.0, in1=mask_rows[:, cols], op0=MAX, op1=MULT
             )
 
             queue = nc.sync if i % 2 == 0 else nc.scalar

@@ -67,5 +67,4 @@ def tile_domleavesembedding_kernel(tc, table, w, wpos, b, mask, offs, out):
                 out=result[:], in0=pres[i][:], scalar=0.0, in1=mask_rows[:, cols], op0=MAX, op1=MULT
             )
 
-            queue = nc.sync if i % 2 == 0 else nc.scalar
-            queue.dma_start(out[:, cols], result[:])
+            nc.sync.dma_start(out[:, cols], result[:])

@@ -1,4 +1,5 @@
 import concourse.mybir as mybir
+from concourse.masks import make_identity
 
 BF16, F32, U16 = mybir.dt.bfloat16, mybir.dt.float32, mybir.dt.uint16
 ADD, MAX, MULT = mybir.AluOpType.add, mybir.AluOpType.max, mybir.AluOpType.mult
@@ -11,7 +12,9 @@ PIECE = 512
 PIECES = N // PIECE
 GOALS = PIECE // POSITIONS
 LANES = 16
-MASK_LOAD = 1024
+BLOCKS = PIECE // P
+BY_LOAD = PIECES // 2
+LOADED = BY_LOAD * PIECE
 
 FLOPS = 2 * P * P * N
 
@@ -22,11 +25,14 @@ def tile_domleavesembedding_kernel(tc, table, w, wpos, b, mask, offs, out):
         tc.tile_pool(name="held", bufs=1) as held,
         tc.tile_pool(name="work", bufs=PIECES) as work,
         tc.psum_pool(name="banks", bufs=PIECES) as banks,
+        tc.psum_pool(name="spread", bufs=PIECES - BY_LOAD) as spread,
     ):
         offsets = held.tile([P, N // LANES], U16, name="offsets")
         nc.sync.dma_start(offsets[:], offs)
         words = held.tile([P, WORDS], BF16, name="words")
         nc.sync.dma_start(words[:], table)
+        mask_rows = held.tile([P, LOADED], F32, name="mask_rows")
+        nc.sync.dma_start(mask_rows[:], mask[:, 0:LOADED].to_broadcast([P, LOADED]))
 
         weights = held.tile([P, P], BF16, name="weights")
         nc.scalar.dma_start(weights[:], w)
@@ -34,11 +40,12 @@ def tile_domleavesembedding_kernel(tc, table, w, wpos, b, mask, offs, out):
         nc.scalar.dma_start(position[:], wpos)
         bias = held.tile([P, 1], F32, name="bias")
         nc.scalar.dma_start(bias[:], b)
+        mask_columns = held.tile([P, PIECES - BY_LOAD, BLOCKS], F32, name="mask_columns")
+        with nc.allow_non_contiguous_dma(reason="runs of four float32 entries of the mask"):
+            nc.scalar.dma_start(mask_columns[:], mask[:, LOADED:N].rearrange("o (i p k) -> p (o i) k", p=P, k=BLOCKS))
 
-        mask_rows = held.tile([P, N], F32, name="mask_rows")
-        for first in range(0, N, MASK_LOAD):
-            cols = slice(first, first + MASK_LOAD)
-            nc.sync.dma_start(mask_rows[:, cols], mask[:, cols].to_broadcast([P, MASK_LOAD]))
+        identity = held.tile([P, P], F32, name="identity")
+        make_identity(nc, identity[:])
 
         position_per_goal = position[:].unsqueeze(1).to_broadcast([P, GOALS, POSITIONS])
 
@@ -62,9 +69,21 @@ def tile_domleavesembedding_kernel(tc, table, w, wpos, b, mask, offs, out):
         for i in range(PIECES):
             cols = slice(i * PIECE, (i + 1) * PIECE)
 
+            if i < BY_LOAD:
+                mask_piece = mask_rows[:, cols]
+            else:
+                spread_rows = spread.tile([P, PIECE], F32, name="spread_rows")
+                for k in range(BLOCKS):
+                    nc.tensor.transpose(
+                        spread_rows[:].rearrange("m (p k) -> m k p", k=BLOCKS)[:, k, :],
+                        mask_columns[:, i - BY_LOAD, k : k + 1].to_broadcast([P, P]),
+                        identity[:],
+                    )
+                mask_piece = spread_rows[:]
+
             result = work.tile([P, PIECE], F32, name="result")
             nc.vector.scalar_tensor_tensor(
-                out=result[:], in0=pres[i][:], scalar=0.0, in1=mask_rows[:, cols], op0=MAX, op1=MULT
+                out=result[:], in0=pres[i][:], scalar=0.0, in1=mask_piece, op0=MAX, op1=MULT
             )
 
             nc.sync.dma_start(out[:, cols], result[:])

import concourse.mybir as mybir
from concourse.masks import make_identity

BF16, F32, U16 = mybir.dt.bfloat16, mybir.dt.float32, mybir.dt.uint16
ADD, MAX, MULT = mybir.AluOpType.add, mybir.AluOpType.max, mybir.AluOpType.mult

P = 128
WORDS = 4096
N = 2048
POSITIONS = 32
PIECE = 512
PIECES = N // PIECE
GOALS = PIECE // POSITIONS
LANES = 16
BLOCKS = PIECE // P
BY_LOAD = PIECES // 2
LOADED = BY_LOAD * PIECE

FLOPS = 2 * P * P * N


def tile_domleavesembedding_kernel(tc, table, w, wpos, b, mask, offs, out):
    nc = tc.nc
    with (
        tc.tile_pool(name="held", bufs=1) as held,
        tc.tile_pool(name="work", bufs=PIECES) as work,
        tc.psum_pool(name="banks", bufs=PIECES) as banks,
        tc.psum_pool(name="spread", bufs=PIECES - BY_LOAD) as spread,
    ):
        offsets = held.tile([P, N // LANES], U16, name="offsets")
        nc.sync.dma_start(offsets[:], offs)
        words = held.tile([P, WORDS], BF16, name="words")
        nc.sync.dma_start(words[:], table)
        mask_rows = held.tile([P, LOADED], F32, name="mask_rows")
        nc.sync.dma_start(mask_rows[:], mask[:, 0:LOADED].to_broadcast([P, LOADED]))

        weights = held.tile([P, P], BF16, name="weights")
        nc.scalar.dma_start(weights[:], w)
        position = held.tile([P, POSITIONS], F32, name="position")
        nc.scalar.dma_start(position[:], wpos)
        bias = held.tile([P, 1], F32, name="bias")
        nc.scalar.dma_start(bias[:], b)
        mask_columns = held.tile([P, PIECES - BY_LOAD, BLOCKS], F32, name="mask_columns")
        with nc.allow_non_contiguous_dma(reason="runs of four float32 entries of the mask"):
            nc.scalar.dma_start(mask_columns[:], mask[:, LOADED:N].rearrange("o (i p k) -> p (o i) k", p=P, k=BLOCKS))

        identity = held.tile([P, P], F32, name="identity")
        make_identity(nc, identity[:])

        position_per_goal = position[:].unsqueeze(1).to_broadcast([P, GOALS, POSITIONS])

        pres = []
        for i in range(PIECES):
            picked = words[:].indirect(offsets[:, i * PIECE // LANES : (i + 1) * PIECE // LANES])
            product = banks.tile([P, PIECE], F32, name="product")
            nc.tensor.matmul(product[:], weights[:], picked, start=True, stop=True)

            pre = work.tile([P, PIECE], F32, name="pre")
            nc.vector.scalar_tensor_tensor(
                out=pre[:].rearrange("p (g t) -> p g t", t=POSITIONS),
                in0=product[:].rearrange("p (g t) -> p g t", t=POSITIONS),
                scalar=bias[:, 0:1],
                in1=position_per_goal,
                op0=ADD,
                op1=ADD,
            )
            pres.append(pre)

        for i in range(PIECES):
            cols = slice(i * PIECE, (i + 1) * PIECE)

            if i < BY_LOAD:
                mask_piece = mask_rows[:, cols]
            else:
                spread_rows = spread.tile([P, PIECE], F32, name="spread_rows")
                for k in range(BLOCKS):
                    nc.tensor.transpose(
                        spread_rows[:].rearrange("m (p k) -> m k p", k=BLOCKS)[:, k, :],
                        mask_columns[:, i - BY_LOAD, k : k + 1].to_broadcast([P, P]),
                        identity[:],
                    )
                mask_piece = spread_rows[:]

            result = work.tile([P, PIECE], F32, name="result")
            nc.vector.scalar_tensor_tensor(
                out=result[:], in0=pres[i][:], scalar=0.0, in1=mask_piece, op0=MAX, op1=MULT
            )

            nc.sync.dma_start(out[:, cols], result[:])
